import numpy as np
import ml_dtypes


def mxq(x, axis, fmt="e4m3"):
    dtype, down = {"e4m3": (ml_dtypes.float8_e4m3fn, 7), "e5m2": (ml_dtypes.float8_e5m2, 14)}[fmt]
    v = np.moveaxis(np.asarray(x, np.float32).astype(ml_dtypes.bfloat16).astype(np.float64), axis, -1)
    blocks = v.reshape(v.shape[:-1] + (-1, 32))
    amax = np.abs(blocks).max(-1, keepdims=True)
    byte = np.maximum(np.where(amax > 0, np.frexp(amax)[1] - 1 + 127, 0) - down, 1)
    scale = np.exp2(byte - 127.0)
    codes = (blocks / scale).astype(np.float32).astype(dtype).astype(np.float64)
    return np.moveaxis((codes * scale).reshape(v.shape), -1, axis)


WIDE = False


def mx_kscale(k):
    if not WIDE:
        return np.ones(k)
    levels = np.array([10, -10, 5, -5, 0])
    a = np.random.permutation(np.resize(levels, k // 512 * 4)).reshape(k // 512, 4)
    idx = np.arange(k)
    return np.exp2(a[idx // 512, idx % 128 // 32])


BF16 = ml_dtypes.bfloat16


def bf(x):
    return np.asarray(x, np.float32).astype(BF16)


def f64(x):
    return np.asarray(x).astype(np.float64)


B, N, DIM, R, KEY = 1, 1024, 1024, 4, 128
UV = DIM * R // 2
WI = DIM * R + KEY


def silu(z):
    return z / (1.0 + np.exp(-z))


def rope_tables(n, d):
    half = d // 2
    omega = 1.0 / (10000.0 ** (np.arange(half) / half))
    ang = np.arange(n)[:, None] * omega[None, :]
    return np.sin(ang), np.cos(ang)


def apply_rotary(x, sin, cos):
    x1, x2 = x[..., 0::2], x[..., 1::2]
    return np.concatenate([x1 * cos - x2 * sin, x1 * sin + x2 * cos], axis=-1)


def setup_inputs():
    s = mx_kscale(DIM)
    return {"hidden_states": bf(np.random.standard_normal((B, N, DIM)) * s),
            "Wi": bf(np.random.standard_normal((DIM, WI)) / np.sqrt(DIM) / s[:, None]),
            "bi": bf(np.random.standard_normal(WI) * 0.1),
            "q_gamma": bf(2.0 + 0.2 * np.random.standard_normal(KEY)),
            "q_beta": bf(0.3 * np.random.standard_normal(KEY)),
            "k_gamma": bf(2.0 + 0.2 * np.random.standard_normal(KEY)),
            "k_beta": bf(0.3 * np.random.standard_normal(KEY))}


def reference(hidden_states, Wi, bi, q_gamma, q_beta, k_gamma, k_beta):
    sin, cos = rope_tables(N, KEY)
    x = silu((mxq(f64(hidden_states), 2, "e4m3") @ mxq(f64(Wi), 0, "e4m3")) + f64(bi))
    u = x[..., :UV]
    v = x[..., UV:2 * UV]
    qk = x[..., 2 * UV:]
    q = apply_rotary(qk * f64(q_gamma) + f64(q_beta), sin, cos)
    k = apply_rotary(qk * f64(k_gamma) + f64(k_beta), sin, cos)
    return u, v, q, k

@@ -1,0 +1,277 @@
+import math
+from contextlib import ExitStack
+
+import concourse.mybir as mybir
+from concourse.masks import make_identity
+
+F32 = mybir.dt.float32
+BF16 = mybir.dt.bfloat16
+I32 = mybir.dt.int32
+U32 = mybir.dt.uint32
+U8 = mybir.dt.uint8
+FP8X4 = mybir.dt.float8_e4m3fn_x4
+ALU = mybir.AluOpType
+ACT = mybir.ActivationFunctionType
+
+P = 128
+TOK = 1024
+DIM = 1024
+UV = 2048
+KEY = 128
+HALF = KEY // 2
+WI = 2 * UV + KEY
+MT = TOK // P
+NG = DIM // 512
+CH = 512
+NVEC = WI // P + 4
+
+ON_SCALAR = ((2, 1), (3, 1), (4, 1), (5, 1), (6, 1), (7, 0), (7, 1))
+
+FLOPS = 2 * TOK * DIM * WI
+
+
+def tile_gau_ae_pa_kernel(
+    tc, hidden_states, Wi, bi, q_gamma, q_beta, k_gamma, k_beta, out_0, out_1, out_2, out_3
+):
+    nc = tc.nc
+    h_dram = hidden_states.flatten_outer_dims().rearrange("(p m) k -> p m k", m=MT)
+    uv_dram = [
+        out_0.flatten_outer_dims().rearrange("(p m) c -> p m c", m=MT),
+        out_1.flatten_outer_dims().rearrange("(p m) c -> p m c", m=MT),
+    ]
+    qk_dram = [
+        out_2.flatten_outer_dims().rearrange("(p m) f -> p (m f)", m=MT),
+        out_3.flatten_outer_dims().rearrange("(p m) f -> p (m f)", m=MT),
+    ]
+
+    with ExitStack() as ctx:
+        const = ctx.enter_context(tc.tile_pool(name="const", bufs=1))
+        rawp = ctx.enter_context(tc.tile_pool(name="rawp", bufs=3))
+        grp = ctx.enter_context(tc.tile_pool(name="grp", bufs=2))
+        stage = ctx.enter_context(tc.tile_pool(name="stage", bufs=4))
+        rot = ctx.enter_context(tc.tile_pool(name="rot", bufs=2))
+        psum = ctx.enter_context(tc.psum_pool(name="psum", bufs=8))
+
+        vecs = const.tile([P, P], BF16, name="vecs")
+        nc.gpsimd.memset(vecs[:], 0.0)
+        nc.sync.dma_start(out=vecs[0 : WI // P, :], in_=bi.rearrange("(r n) -> r n", n=P))
+        for i, v in enumerate((q_gamma, q_beta, k_gamma, k_beta)):
+            r = WI // P + i
+            nc.sync.dma_start(out=vecs[r : r + 1, :], in_=v.rearrange("(o n) -> o n", o=1))
+        ident_bf = const.tile([P, P], BF16, name="ident_bf")
+        make_identity(nc, ident_bf[:])
+        pos = const.tile([P, MT], F32, name="pos")
+        nc.gpsimd.iota(
+            pos[:], pattern=[[1, MT]], base=0, channel_multiplier=MT,
+            allow_small_or_imprecise_dtypes=True,
+        )
+        ident = const.tile([P, P], F32, name="ident")
+        make_identity(nc, ident[:])
+
+        blocks = [(0, 1024), (1024, 1024), (2048, 1024), (3072, 1152)]
+        raws = []
+
+        def load_block(b):
+            c0, width = blocks[b]
+            for g in range(NG):
+                for u in range(2):
+                    r0 = 512 * g + 256 * u
+                    nc.sync.dma_start(
+                        out=raws[b][:, g, 2 * u : 2 * u + 2, :],
+                        in_=Wi[r0 : r0 + 256, c0 : c0 + width].rearrange("(q e) c -> q e c", e=2),
+                    )
+
+        raw0 = rawp.tile([P, NG, 4, 1024], BF16, name="raw0", tag="rawa")
+        raws.append(raw0)
+        load_block(0)
+        h_half = []
+        for i in range(2):
+            hh = stage.tile([P, MT // 2, DIM], BF16, name="hh%d" % i, tag="st")
+            nc.sync.dma_start(out=hh[:], in_=h_dram[:, 4 * i : 4 * i + 4, :])
+            h_half.append(hh)
+        raw1 = rawp.tile([P, NG, 4, 1024], BF16, name="raw1", tag="rawa")
+        raws.append(raw1)
+        load_block(1)
+        raw2 = rawp.tile([P, NG, 4, 1024], BF16, name="raw2", tag="rawa")
+        raws.append(raw2)
+        load_block(2)
+        raw3 = rawp.tile([P, NG, 4, 1152], BF16, name="raw3", tag="rawb", bufs=1)
+        raws.append(raw3)
+        load_block(3)
+
+        omega = const.tile([P, HALF], F32, name="omega")
+        nc.vector.memset(omega[:, 0:1], 1.0)
+        ratio = 10000.0 ** (-1.0 / HALF)
+        for i in range(6):
+            n = 2 ** i
+            nc.vector.tensor_scalar(
+                out=omega[:, n : 2 * n], in0=omega[:, 0:n], scalar1=ratio ** n, scalar2=None,
+                op0=ALU.mult,
+            )
+        turns = const.tile([P, MT, HALF], F32, name="turns")
+        nc.vector.scalar_tensor_tensor(
+            out=turns[:],
+            in0=omega[:].unsqueeze(1).to_broadcast([P, MT, HALF]),
+            scalar=1.0 / (2.0 * math.pi),
+            in1=pos[:].unsqueeze(2).to_broadcast([P, MT, HALF]),
+            op0=ALU.mult, op1=ALU.mult,
+        )
+        whole_i = const.tile([P, MT, HALF], I32, name="whole_i")
+        nc.vector.tensor_copy(out=whole_i[:], in_=turns[:])
+        whole = const.tile([P, MT, HALF], F32, name="whole")
+        nc.vector.tensor_copy(out=whole[:], in_=whole_i[:])
+        nc.vector.tensor_tensor(out=turns[:], in0=turns[:], in1=whole[:], op=ALU.subtract)
+        negf = whole
+        nc.vector.scalar_tensor_tensor(
+            out=negf[:], in0=turns[:], scalar=0.5, in1=turns[:], op0=ALU.is_gt, op1=ALU.subtract,
+        )
+        sin_t = const.tile([P, MT, HALF], F32, name="sin_t")
+        nc.scalar.activation(out=sin_t[:], in_=negf[:], func=ACT.Sin, scale=-2.0 * math.pi)
+        half_s = turns
+        nc.scalar.activation(out=half_s[:], in_=negf[:], func=ACT.Sin, scale=math.pi)
+        nc.scalar.activation(out=half_s[:], in_=half_s[:], func=ACT.Square)
+        cos_t = const.tile([P, MT, HALF], F32, name="cos_t")
+        nc.gpsimd.tensor_scalar(
+            out=cos_t[:], in0=half_s[:], scalar1=-2.0, scalar2=1.0, op0=ALU.mult, op1=ALU.add,
+        )
+
+        spread = const.tile([P, NVEC * P], BF16, name="spread")
+        for b0 in range(0, NVEC, 8):
+            n = min(8, NVEC - b0)
+            bank_bf = psum.tile([P, 8 * P], BF16, name="bank_bf", tag="bank")
+            for r in range(b0, b0 + n):
+                nc.tensor.matmul(
+                    out=bank_bf[:, (r - b0) * P : (r - b0 + 1) * P],
+                    lhsT=ident_bf[:, r : r + 1].to_broadcast([P, P]),
+                    rhs=vecs[:],
+                    start=True, stop=True,
+                )
+            nc.scalar.copy(out=spread[:, b0 * P : (b0 + n) * P], in_=bank_bf[:, 0 : n * P])
+
+        wc = const.tile([P, NG, WI], U32, name="wc", align_bytes=64)
+        ws = const.tile([P, NG, WI], U8, name="ws", align_bytes=64)
+
+        def prep(c0, width):
+            b = min(c0 // 1024, 3)
+            off = c0 - blocks[b][0]
+            grouped = []
+            for g in range(NG):
+                on_scalar = (c0 // CH, g) in ON_SCALAR
+                tag = "grs" if on_scalar else "grv"
+                gr = grp.tile([P, width, 4], BF16, name="gr%d" % g, tag=tag, align_bytes=64)
+                dst = gr[:].rearrange("p (c i) t -> p c t i", i=4)
+                src = raws[b][:, g, :, off : off + width].rearrange("p t (c i) -> p c t i", i=4)
+                if on_scalar:
+                    nc.scalar.copy(out=dst, in_=src)
+                else:
+                    nc.vector.tensor_copy(out=dst, in_=src)
+                grouped.append(gr)
+            for g in range(NG):
+                nc.vector.quantize_mx(
+                    out=wc[:, g, c0 : c0 + width].bitcast(FP8X4),
+                    scales=ws[:, g, c0 : c0 + width],
+                    in_=grouped[g][:].rearrange("p c t -> p (c t)"),
+                )
+
+        prep(0, CH)
+        prep(CH, CH)
+
+        hc = const.tile([P, MT, NG, P], U32, name="hc", align_bytes=64)
+        hs = const.tile([P, MT, NG, P], U8, name="hs", align_bytes=64)
+        for pair in range(MT // 2):
+            hg = grp.tile([P, 2, NG, P, 4], BF16, name="hg", align_bytes=64)
+            for i in range(2):
+                m = 2 * pair + i
+                xt = psum.tile([P, 2 * NG, P], F32, name="xt", tag="bank")
+                words = h_half[m // 4][:, m % 4, :].bitcast(F32)
+                for s in range(2 * NG):
+                    nc.tensor.transpose(xt[:, s, :], words[:, s * P : (s + 1) * P], ident[:])
+                nc.scalar.copy(
+                    out=hg[:, i].bitcast(F32),
+                    in_=xt[:].rearrange("p (g u) r -> p g r u", u=2),
+                )
+            nc.vector.quantize_mx(
+                out=hc[:, 2 * pair : 2 * pair + 2].rearrange("p m g r -> p (m g r)").bitcast(FP8X4),
+                scales=hs[:, 2 * pair : 2 * pair + 2].rearrange("p m g r -> p (m g r)"),
+                in_=hg[:].rearrange("p i g r t -> p (i g r t)"),
+            )
+
+        for c in range(2, 8):
+            prep(c * CH, CH)
+        prep(2 * UV, KEY)
+
+        def mx_group(acc, m, c0, width):
+            for g in range(NG):
+                nc.tensor.matmul_mx(
+                    out=acc,
+                    lhsT=hc[:, m, g, :].bitcast(FP8X4),
+                    lhsT_scale=hs[:, m, g, :],
+                    rhs=wc[:, g, c0 : c0 + width].bitcast(FP8X4),
+                    rhs_scale=ws[:, g, c0 : c0 + width],
+                    start=(g == 0),
+                    stop=(g == NG - 1),
+                )
+
+        def step(sc, m, pieces):
+            st = stage.tile([P, UV], F32, name="st", tag="st")
+            per = (UV // CH) // pieces
+            for b in range(UV // CH):
+                c0 = sc * UV + b * CH
+                acc = psum.tile([P, CH], F32, name="acc", tag="bank")
+                mx_group(acc[:], m, c0, CH)
+                nc.vector.tensor_tensor(
+                    out=st[:, b * CH : (b + 1) * CH], in0=acc[:], in1=spread[:, c0 : c0 + CH],
+                    op=ALU.add,
+                )
+                if (b + 1) % per == 0:
+                    cols = slice((b + 1 - per) * CH, (b + 1) * CH)
+                    nc.scalar.activation(out=st[:, cols], in_=st[:, cols], func=ACT.Silu)
+                    nc.sync.dma_start(out=uv_dram[sc][:, m, cols], in_=st[:, cols])
+
+        qk_s = const.tile([P, MT, KEY], F32, name="qk_s")
+        ro = const.tile([P, 2, MT, KEY], F32, name="ro")
+        gains = spread[:, WI : WI + 4 * P].rearrange("p (s w f) -> p s w f", s=2, w=2)
+        for h in range(2):
+            ms = slice(4 * h, 4 * h + 4)
+            qp = psum.tile([P, 4, KEY], F32, name="qp", tag="bank")
+            for i in range(4):
+                mx_group(qp[:, i, :], 4 * h + i, 2 * UV, KEY)
+            nc.vector.tensor_tensor(
+                out=qk_s[:, ms, :], in0=qp[:],
+                in1=spread[:, 2 * UV : WI].unsqueeze(1).to_broadcast([P, 4, KEY]),
+                op=ALU.add,
+            )
+            nc.scalar.activation(out=qk_s[:, ms, :], in_=qk_s[:, ms, :], func=ACT.Silu)
+            lin = rot.tile([P, 4, 2, KEY], F32, name="lin")
+            nc.gpsimd.tensor_tensor(
+                out=lin[:],
+                in0=qk_s[:, ms, :].unsqueeze(2).to_broadcast([P, 4, 2, KEY]),
+                in1=gains[:, :, 0, :].unsqueeze(1).to_broadcast([P, 4, 2, KEY]),
+                op=ALU.mult,
+            )
+            nc.gpsimd.tensor_tensor(
+                out=lin[:], in0=lin[:],
+                in1=gains[:, :, 1, :].unsqueeze(1).to_broadcast([P, 4, 2, KEY]),
+                op=ALU.add,
+            )
+            pairs = lin[:].rearrange("p m s (j e) -> p m s j e", e=2)
+            ev = pairs[:, :, :, :, 0]
+            od = pairs[:, :, :, :, 1]
+            cs = cos_t[:, ms, :].unsqueeze(2).to_broadcast([P, 4, 2, HALF])
+            sn = sin_t[:, ms, :].unsqueeze(2).to_broadcast([P, 4, 2, HALF])
+            lo = ro[:, :, ms, 0:HALF].rearrange("p s m j -> p m s j")
+            hi = ro[:, :, ms, HALF:KEY].rearrange("p s m j -> p m s j")
+            t1 = rot.tile([P, 4, 2, HALF], F32, name="t1")
+            t2 = rot.tile([P, 4, 2, HALF], F32, name="t2")
+            nc.gpsimd.tensor_tensor(out=lo, in0=ev, in1=cs, op=ALU.mult)
+            nc.gpsimd.tensor_tensor(out=t1[:], in0=od, in1=sn, op=ALU.mult)
+            nc.gpsimd.tensor_tensor(out=lo, in0=lo, in1=t1[:], op=ALU.subtract)
+            nc.gpsimd.tensor_tensor(out=hi, in0=ev, in1=sn, op=ALU.mult)
+            nc.gpsimd.tensor_tensor(out=t2[:], in0=od, in1=cs, op=ALU.mult)
+            nc.gpsimd.tensor_tensor(out=hi, in0=hi, in1=t2[:], op=ALU.add)
+        for s in range(2):
+            nc.gpsimd.dma_start(out=qk_dram[s], in_=ro[:, s].rearrange("p m f -> p (m f)"))
+
+        for sc in range(2):
+            for m in range(MT):
+                step(sc, m, 4 if (sc == 1 and m == MT - 1) else 1)

@@ -23,11 +23,148 @@ WI = 2 * UV + KEY
 MT = TOK // P
 NG = DIM // 512
 CH = 512
+BLK = 1024
 NVEC = WI // P + 4
 
-ON_SCALAR = ((2, 1), (3, 1), (4, 1), (5, 1), (6, 1), (7, 0), (7, 1))
-
 FLOPS = 2 * TOK * DIM * WI
+
+PINNED = True
+
+ORDER = (
+    ("head",),
+    ("warmSin",),
+    ("ldW", 0, 0),
+    ("ldW", 0, 1),
+    ("ldH", 0),
+    ("ldH", 1),
+    ("ldW", 1, 0),
+    ("ldW", 1, 1),
+    ("ldW", 2, 0),
+    ("ldW", 2, 1),
+    ("ldW", 3, 0),
+    ("ldW", 3, 1),
+    ("tabV",),
+    ("biasM",),
+    ("bc", 0),
+    ("bc", 1),
+    ("bc", 2),
+    ("bc", 3),
+    ("bc", 4),
+    ("tabS",),
+    ("warmSilu",),
+    ("cp", 0, 0, "V"),
+    ("cp", 1, 0, "V"),
+    ("q", 0, 0),
+    ("q", 1, 0),
+    ("cp", 0, 1, "V"),
+    ("cp", 1, 1, "V"),
+    ("q", 0, 1),
+    ("q", 1, 1),
+    ("trH", 0),
+    ("trH", 1),
+    ("trH", 2),
+    ("trH", 3),
+    ("exH", 0),
+    ("exH", 1),
+    ("qH", 0),
+    ("exH", 2),
+    ("exH", 3),
+    ("qH", 1),
+    ("trH", 4),
+    ("trH", 5),
+    ("trH", 6),
+    ("trH", 7),
+    ("exH", 4),
+    ("exH", 5),
+    ("qH", 2),
+    ("exH", 6),
+    ("exH", 7),
+    ("qH", 3),
+    ("mx", 0, 0),
+    ("mx", 0, 1),
+    ("add", 0, 0),
+    ("mx", 0, 2),
+    ("cp", 2, 1, "S"),
+    ("cp", 3, 1, "S"),
+    ("cp", 2, 0, "V"),
+    ("cp", 3, 0, "V"),
+    ("q", 2, 0),
+    ("q", 3, 0),
+    ("silu", 0, 0, 1),
+    ("add", 0, 1),
+    ("mx", 0, 3),
+    ("q", 2, 1),
+    ("q", 3, 1),
+    ("cp", 4, 1, "S"),
+    ("cp", 5, 1, "S"),
+    ("cp", 4, 0, "V"),
+    ("cp", 5, 0, "V"),
+    ("q", 4, 0),
+    ("q", 5, 0),
+    ("silu", 0, 1, 1),
+    ("add", 0, 2),
+    ("mx", 1, 0),
+    ("q", 4, 1),
+    ("q", 5, 1),
+    ("cp", 6, 1, "S"),
+    ("cp", 7, 1, "S"),
+    ("cp", 6, 0, "V"),
+    ("cp", 7, 0, "V"),
+    ("q", 6, 0),
+    ("q", 7, 0),
+    ("silu", 0, 2, 1),
+    ("add", 0, 3),
+    ("cp", 8, 0, "V"),
+    ("cp", 8, 1, "V"),
+    ("q", 6, 1),
+    ("q", 7, 1),
+    ("q", 8, 0),
+    ("q", 8, 1),
+    ("mxq", 0),
+    ("mxq", 1),
+    ("addq", 0),
+    ("addq", 1),
+    ("silu", 0, 3, 1),
+    ("siluq", 0),
+    ("rot", 0),
+    ("siluq", 1),
+    ("rot", 1),
+    ("add", 1, 0),
+    ("mx", 1, 1),
+    ("mx", 1, 2),
+    ("silu", 1, 0, 1),
+    ("add", 1, 1),
+    ("mx", 1, 3),
+    ("silu", 1, 1, 1),
+    ("add", 1, 2),
+    ("mx", 2, 0),
+    ("silu", 1, 2, 1),
+    ("add", 1, 3),
+    ("mx", 2, 1),
+    ("silu", 1, 3, 1),
+    ("add", 2, 0),
+    ("mx", 2, 2),
+    ("silu", 2, 0, 1),
+    ("add", 2, 1),
+    ("mx", 2, 3),
+    ("silu", 2, 1, 1),
+    ("add", 2, 2),
+    ("mx", 3, 0),
+    ("silu", 2, 2, 1),
+    ("add", 2, 3),
+    ("mx", 3, 1),
+    ("silu", 2, 3, 1),
+    ("add", 3, 0),
+    ("mx", 3, 2),
+    ("silu", 3, 0, 1),
+    ("add", 3, 1),
+    ("mx", 3, 3),
+    ("silu", 3, 1, 1),
+    ("add", 3, 2),
+    ("silu", 3, 2, 1),
+    ("add", 3, 3),
+    ("silu", 3, 3, 4),
+)
 
 
 def tile_gau_ae_pa_kernel(
@@ -43,6 +180,7 @@ def tile_gau_ae_pa_kernel(
         out_2.flatten_outer_dims().rearrange("(p m) f -> p (m f)", m=MT),
         out_3.flatten_outer_dims().rearrange("(p m) f -> p (m f)", m=MT),
     ]
+    blocks = [(0, 1024), (1024, 1024), (2048, 1024), (3072, 1152)]
 
     with ExitStack() as ctx:
         const = ctx.enter_context(tc.tile_pool(name="const", bufs=1))
@@ -51,154 +189,165 @@ def tile_gau_ae_pa_kernel(
         stage = ctx.enter_context(tc.tile_pool(name="stage", bufs=4))
         rot = ctx.enter_context(tc.tile_pool(name="rot", bufs=2))
         psum = ctx.enter_context(tc.psum_pool(name="psum", bufs=8))
+        if PINNED:
+            ctx.enter_context(tc.manual_schedule())
 
         vecs = const.tile([P, P], BF16, name="vecs")
-        nc.gpsimd.memset(vecs[:], 0.0)
-        nc.sync.dma_start(out=vecs[0 : WI // P, :], in_=bi.rearrange("(r n) -> r n", n=P))
-        for i, v in enumerate((q_gamma, q_beta, k_gamma, k_beta)):
-            r = WI // P + i
-            nc.sync.dma_start(out=vecs[r : r + 1, :], in_=v.rearrange("(o n) -> o n", o=1))
         ident_bf = const.tile([P, P], BF16, name="ident_bf")
-        make_identity(nc, ident_bf[:])
-        pos = const.tile([P, MT], F32, name="pos")
-        nc.gpsimd.iota(
-            pos[:], pattern=[[1, MT]], base=0, channel_multiplier=MT,
-            allow_small_or_imprecise_dtypes=True,
-        )
         ident = const.tile([P, P], F32, name="ident")
-        make_identity(nc, ident[:])
-
-        blocks = [(0, 1024), (1024, 1024), (2048, 1024), (3072, 1152)]
-        raws = []
-
-        def load_block(b):
-            c0, width = blocks[b]
-            for g in range(NG):
-                for u in range(2):
-                    r0 = 512 * g + 256 * u
-                    nc.sync.dma_start(
-                        out=raws[b][:, g, 2 * u : 2 * u + 2, :],
-                        in_=Wi[r0 : r0 + 256, c0 : c0 + width].rearrange("(q e) c -> q e c", e=2),
-                    )
-
-        raw0 = rawp.tile([P, NG, 4, 1024], BF16, name="raw0", tag="rawa")
-        raws.append(raw0)
-        load_block(0)
-        h_half = []
-        for i in range(2):
-            hh = stage.tile([P, MT // 2, DIM], BF16, name="hh%d" % i, tag="st")
-            nc.sync.dma_start(out=hh[:], in_=h_dram[:, 4 * i : 4 * i + 4, :])
-            h_half.append(hh)
-        raw1 = rawp.tile([P, NG, 4, 1024], BF16, name="raw1", tag="rawa")
-        raws.append(raw1)
-        load_block(1)
-        raw2 = rawp.tile([P, NG, 4, 1024], BF16, name="raw2", tag="rawa")
-        raws.append(raw2)
-        load_block(2)
-        raw3 = rawp.tile([P, NG, 4, 1152], BF16, name="raw3", tag="rawb", bufs=1)
-        raws.append(raw3)
-        load_block(3)
-
+        pos = const.tile([P, MT], F32, name="pos")
         omega = const.tile([P, HALF], F32, name="omega")
-        nc.vector.memset(omega[:, 0:1], 1.0)
-        ratio = 10000.0 ** (-1.0 / HALF)
-        for i in range(6):
-            n = 2 ** i
-            nc.vector.tensor_scalar(
-                out=omega[:, n : 2 * n], in0=omega[:, 0:n], scalar1=ratio ** n, scalar2=None,
-                op0=ALU.mult,
-            )
         turns = const.tile([P, MT, HALF], F32, name="turns")
-        nc.vector.scalar_tensor_tensor(
-            out=turns[:],
-            in0=omega[:].unsqueeze(1).to_broadcast([P, MT, HALF]),
-            scalar=1.0 / (2.0 * math.pi),
-            in1=pos[:].unsqueeze(2).to_broadcast([P, MT, HALF]),
-            op0=ALU.mult, op1=ALU.mult,
-        )
         whole_i = const.tile([P, MT, HALF], I32, name="whole_i")
-        nc.vector.tensor_copy(out=whole_i[:], in_=turns[:])
         whole = const.tile([P, MT, HALF], F32, name="whole")
-        nc.vector.tensor_copy(out=whole[:], in_=whole_i[:])
-        nc.vector.tensor_tensor(out=turns[:], in0=turns[:], in1=whole[:], op=ALU.subtract)
-        negf = whole
-        nc.vector.scalar_tensor_tensor(
-            out=negf[:], in0=turns[:], scalar=0.5, in1=turns[:], op0=ALU.is_gt, op1=ALU.subtract,
-        )
         sin_t = const.tile([P, MT, HALF], F32, name="sin_t")
-        nc.scalar.activation(out=sin_t[:], in_=negf[:], func=ACT.Sin, scale=-2.0 * math.pi)
-        half_s = turns
-        nc.scalar.activation(out=half_s[:], in_=negf[:], func=ACT.Sin, scale=math.pi)
-        nc.scalar.activation(out=half_s[:], in_=half_s[:], func=ACT.Square)
         cos_t = const.tile([P, MT, HALF], F32, name="cos_t")
-        nc.gpsimd.tensor_scalar(
-            out=cos_t[:], in0=half_s[:], scalar1=-2.0, scalar2=1.0, op0=ALU.mult, op1=ALU.add,
-        )
-
         spread = const.tile([P, NVEC * P], BF16, name="spread")
-        for b0 in range(0, NVEC, 8):
-            n = min(8, NVEC - b0)
-            bank_bf = psum.tile([P, 8 * P], BF16, name="bank_bf", tag="bank")
-            for r in range(b0, b0 + n):
-                nc.tensor.matmul(
-                    out=bank_bf[:, (r - b0) * P : (r - b0 + 1) * P],
-                    lhsT=ident_bf[:, r : r + 1].to_broadcast([P, P]),
-                    rhs=vecs[:],
-                    start=True, stop=True,
-                )
-            nc.scalar.copy(out=spread[:, b0 * P : (b0 + n) * P], in_=bank_bf[:, 0 : n * P])
-
         wc = const.tile([P, NG, WI], U32, name="wc", align_bytes=64)
         ws = const.tile([P, NG, WI], U8, name="ws", align_bytes=64)
-
-        def prep(c0, width):
-            b = min(c0 // 1024, 3)
-            off = c0 - blocks[b][0]
-            grouped = []
-            for g in range(NG):
-                on_scalar = (c0 // CH, g) in ON_SCALAR
-                tag = "grs" if on_scalar else "grv"
-                gr = grp.tile([P, width, 4], BF16, name="gr%d" % g, tag=tag, align_bytes=64)
-                dst = gr[:].rearrange("p (c i) t -> p c t i", i=4)
-                src = raws[b][:, g, :, off : off + width].rearrange("p t (c i) -> p c t i", i=4)
-                if on_scalar:
-                    nc.scalar.copy(out=dst, in_=src)
-                else:
-                    nc.vector.tensor_copy(out=dst, in_=src)
-                grouped.append(gr)
-            for g in range(NG):
-                nc.vector.quantize_mx(
-                    out=wc[:, g, c0 : c0 + width].bitcast(FP8X4),
-                    scales=ws[:, g, c0 : c0 + width],
-                    in_=grouped[g][:].rearrange("p c t -> p (c t)"),
-                )
-
-        prep(0, CH)
-        prep(CH, CH)
-
         hc = const.tile([P, MT, NG, P], U32, name="hc", align_bytes=64)
         hs = const.tile([P, MT, NG, P], U8, name="hs", align_bytes=64)
-        for pair in range(MT // 2):
-            hg = grp.tile([P, 2, NG, P, 4], BF16, name="hg", align_bytes=64)
-            for i in range(2):
-                m = 2 * pair + i
-                xt = psum.tile([P, 2 * NG, P], F32, name="xt", tag="bank")
-                words = h_half[m // 4][:, m % 4, :].bitcast(F32)
-                for s in range(2 * NG):
-                    nc.tensor.transpose(xt[:, s, :], words[:, s * P : (s + 1) * P], ident[:])
-                nc.scalar.copy(
-                    out=hg[:, i].bitcast(F32),
-                    in_=xt[:].rearrange("p (g u) r -> p g r u", u=2),
+        qk_s = const.tile([P, MT, KEY], F32, name="qk_s")
+        ro = const.tile([P, 2, MT, KEY], F32, name="ro")
+        gains = spread[:, WI : WI + 4 * P].rearrange("p (s w f) -> p s w f", s=2, w=2)
+
+        scrap_in = const.tile([P, 1], F32, name="scrap_in")
+        scrap_out = const.tile([P, 1], F32, name="scrap_out")
+
+        live = {}
+
+        def head():
+            nc.gpsimd.memset(scrap_in[:], 0.0)
+            nc.gpsimd.memset(vecs[:], 0.0)
+            nc.sync.dma_start(out=vecs[0 : WI // P, :], in_=bi.rearrange("(r n) -> r n", n=P))
+            for i, v in enumerate((q_gamma, q_beta, k_gamma, k_beta)):
+                r = WI // P + i
+                nc.sync.dma_start(out=vecs[r : r + 1, :], in_=v.rearrange("(o n) -> o n", o=1))
+            make_identity(nc, ident_bf[:])
+            nc.gpsimd.iota(
+                pos[:], pattern=[[1, MT]], base=0, channel_multiplier=MT,
+                allow_small_or_imprecise_dtypes=True,
+            )
+            make_identity(nc, ident[:])
+
+        def warm(func):
+            nc.scalar.activation(out=scrap_out[:], in_=scrap_in[:], func=func)
+
+        def load_w(b, g):
+            c0, width = blocks[b]
+            if ("raw", b) not in live:
+                if b < 3:
+                    raw = rawp.tile([P, NG, 4, width], BF16, name="raw%d" % b, tag="rawa")
+                else:
+                    raw = rawp.tile([P, NG, 4, width], BF16, name="raw%d" % b, tag="rawb", bufs=1)
+                live[("raw", b)] = raw
+            raw = live[("raw", b)]
+            for u in range(2):
+                r0 = 512 * g + 256 * u
+                nc.sync.dma_start(
+                    out=raw[:, g, 2 * u : 2 * u + 2, :],
+                    in_=Wi[r0 : r0 + 256, c0 : c0 + width].rearrange("(q e) c -> q e c", e=2),
                 )
-            nc.vector.quantize_mx(
-                out=hc[:, 2 * pair : 2 * pair + 2].rearrange("p m g r -> p (m g r)").bitcast(FP8X4),
-                scales=hs[:, 2 * pair : 2 * pair + 2].rearrange("p m g r -> p (m g r)"),
-                in_=hg[:].rearrange("p i g r t -> p (i g r t)"),
+
+        def load_h(i):
+            hh = stage.tile([P, MT // 2, DIM], BF16, name="hh%d" % i, tag="st")
+            nc.sync.dma_start(out=hh[:], in_=h_dram[:, 4 * i : 4 * i + 4, :])
+            live[("hh", i)] = hh
+
+        def tab_v():
+            nc.vector.memset(omega[:, 0:1], 1.0)
+            ratio = 10000.0 ** (-1.0 / HALF)
+            for i in range(6):
+                n = 2 ** i
+                nc.vector.tensor_scalar(
+                    out=omega[:, n : 2 * n], in0=omega[:, 0:n], scalar1=ratio ** n, scalar2=None,
+                    op0=ALU.mult,
+                )
+            nc.vector.scalar_tensor_tensor(
+                out=turns[:],
+                in0=omega[:].unsqueeze(1).to_broadcast([P, MT, HALF]),
+                scalar=1.0 / (2.0 * math.pi),
+                in1=pos[:].unsqueeze(2).to_broadcast([P, MT, HALF]),
+                op0=ALU.mult, op1=ALU.mult,
+            )
+            nc.vector.tensor_copy(out=whole_i[:], in_=turns[:])
+            nc.vector.tensor_copy(out=whole[:], in_=whole_i[:])
+            nc.vector.tensor_tensor(out=turns[:], in0=turns[:], in1=whole[:], op=ALU.subtract)
+            nc.vector.scalar_tensor_tensor(
+                out=whole[:], in0=turns[:], scalar=0.5, in1=turns[:], op0=ALU.is_gt,
+                op1=ALU.subtract,
             )
 
-        for c in range(2, 8):
-            prep(c * CH, CH)
-        prep(2 * UV, KEY)
+        def tab_s():
+            nc.scalar.activation(out=sin_t[:], in_=whole[:], func=ACT.Sin, scale=-2.0 * math.pi)
+            nc.scalar.activation(out=turns[:], in_=whole[:], func=ACT.Sin, scale=math.pi)
+            nc.scalar.activation(out=turns[:], in_=turns[:], func=ACT.Square)
+            nc.gpsimd.tensor_scalar(
+                out=cos_t[:], in0=turns[:], scalar1=-2.0, scalar2=1.0, op0=ALU.mult, op1=ALU.add,
+            )
+
+        def bias_m():
+            for i in range(5):
+                n = min(8, NVEC - 8 * i)
+                bank_bf = psum.tile([P, 8 * P], BF16, name="bank_bf", tag="bank")
+                for r in range(n):
+                    nc.tensor.matmul(
+                        out=bank_bf[:, r * P : (r + 1) * P],
+                        lhsT=ident_bf[:, 8 * i + r : 8 * i + r + 1].to_broadcast([P, P]),
+                        rhs=vecs[:],
+                        start=True, stop=True,
+                    )
+                live[("bb", i)] = bank_bf
+
+        def bias_c(i):
+            n = min(8, NVEC - 8 * i)
+            nc.scalar.copy(
+                out=spread[:, 8 * i * P : (8 * i + n) * P], in_=live[("bb", i)][:, 0 : n * P]
+            )
+
+        def tr_h(m):
+            xt = psum.tile([P, 2 * NG, P], F32, name="xt", tag="bank")
+            words = live[("hh", m // 4)][:, m % 4, :].bitcast(F32)
+            for s in range(2 * NG):
+                nc.tensor.transpose(xt[:, s, :], words[:, s * P : (s + 1) * P], ident[:])
+            live[("xt", m)] = xt
+
+        def ex_h(m):
+            if ("hg", m // 2) not in live:
+                hg = grp.tile([P, 2, NG, P, 4], BF16, name="hg", align_bytes=64)
+                live[("hg", m // 2)] = hg
+            nc.scalar.copy(
+                out=live[("hg", m // 2)][:, m % 2].bitcast(F32),
+                in_=live[("xt", m)][:].rearrange("p (g u) r -> p g r u", u=2),
+            )
+
+        def q_h(pr):
+            nc.vector.quantize_mx(
+                out=hc[:, 2 * pr : 2 * pr + 2].rearrange("p m g r -> p (m g r)").bitcast(FP8X4),
+                scales=hs[:, 2 * pr : 2 * pr + 2].rearrange("p m g r -> p (m g r)"),
+                in_=live[("hg", pr)][:].rearrange("p i g r t -> p (i g r t)"),
+            )
+
+        def cp(c, g, eng):
+            width = KEY if c == 8 else CH
+            b = min(c // 2, 3)
+            off = c * CH - blocks[b][0]
+            gr = grp.tile([P, width, 4], BF16, name="gr", tag="gr" + eng, align_bytes=64)
+            dst = gr[:].rearrange("p (c i) t -> p c t i", i=4)
+            src = live[("raw", b)][:, g, :, off : off + width].rearrange("p t (c i) -> p c t i", i=4)
+            if eng == "S":
+                nc.scalar.copy(out=dst, in_=src)
+            else:
+                nc.vector.tensor_copy(out=dst, in_=src)
+            live[("gr", c, g)] = gr
+
+        def quant(c, g):
+            width = KEY if c == 8 else CH
+            nc.vector.quantize_mx(
+                out=wc[:, g, c * CH : c * CH + width].bitcast(FP8X4),
+                scales=ws[:, g, c * CH : c * CH + width],
+                in_=live[("gr", c, g)][:].rearrange("p c t -> p (c t)"),
+            )
 
         def mx_group(acc, m, c0, width):
             for g in range(NG):
@@ -212,36 +361,62 @@ def tile_gau_ae_pa_kernel(
                     stop=(g == NG - 1),
                 )
 
-        def step(sc, m, pieces):
-            st = stage.tile([P, UV], F32, name="st", tag="st")
-            per = (UV // CH) // pieces
-            for b in range(UV // CH):
-                c0 = sc * UV + b * CH
+        def mx(bl, pr):
+            for k in range(4):
                 acc = psum.tile([P, CH], F32, name="acc", tag="bank")
-                mx_group(acc[:], m, c0, CH)
-                nc.vector.tensor_tensor(
-                    out=st[:, b * CH : (b + 1) * CH], in0=acc[:], in1=spread[:, c0 : c0 + CH],
-                    op=ALU.add,
-                )
-                if (b + 1) % per == 0:
-                    cols = slice((b + 1 - per) * CH, (b + 1) * CH)
-                    nc.scalar.activation(out=st[:, cols], in_=st[:, cols], func=ACT.Silu)
-                    nc.sync.dma_start(out=uv_dram[sc][:, m, cols], in_=st[:, cols])
+                mx_group(acc[:], 2 * pr + k // 2, bl * BLK + (k % 2) * CH, CH)
+                live[("acc", bl, pr, k)] = acc
 
-        qk_s = const.tile([P, MT, KEY], F32, name="qk_s")
-        ro = const.tile([P, 2, MT, KEY], F32, name="ro")
-        gains = spread[:, WI : WI + 4 * P].rearrange("p (s w f) -> p s w f", s=2, w=2)
-        for h in range(2):
-            ms = slice(4 * h, 4 * h + 4)
+        def add(bl, pr):
+            st = stage.tile([P, 2, BLK], F32, name="st", tag="st")
+            live[("st", bl, pr)] = st
+            for k in range(4):
+                c0 = bl * BLK + (k % 2) * CH
+                nc.vector.tensor_tensor(
+                    out=st[:, k // 2, (k % 2) * CH : (k % 2 + 1) * CH],
+                    in0=live[("acc", bl, pr, k)][:], in1=spread[:, c0 : c0 + CH], op=ALU.add,
+                )
+
+        def silu(bl, pr, pieces):
+            st = live[("st", bl, pr)]
+            dst = uv_dram[bl // 2]
+            off = (bl % 2) * BLK
+            if pieces == 1:
+                nc.scalar.activation(out=st[:], in_=st[:], func=ACT.Silu)
+                nc.sync.dma_start(out=dst[:, 2 * pr : 2 * pr + 2, off : off + BLK], in_=st[:])
+            else:
+                w = 2 * BLK // pieces
+                for i in range(pieces):
+                    row = (i * w) // BLK
+                    col = (i * w) % BLK
+                    nc.scalar.activation(
+                        out=st[:, row, col : col + w], in_=st[:, row, col : col + w], func=ACT.Silu
+                    )
+                    nc.sync.dma_start(
+                        out=dst[:, 2 * pr + row, off + col : off + col + w],
+                        in_=st[:, row, col : col + w],
+                    )
+
+        def mxq(h):
             qp = psum.tile([P, 4, KEY], F32, name="qp", tag="bank")
             for i in range(4):
                 mx_group(qp[:, i, :], 4 * h + i, 2 * UV, KEY)
+            live[("qp", h)] = qp
+
+        def addq(h):
             nc.vector.tensor_tensor(
-                out=qk_s[:, ms, :], in0=qp[:],
+                out=qk_s[:, 4 * h : 4 * h + 4, :], in0=live[("qp", h)][:],
                 in1=spread[:, 2 * UV : WI].unsqueeze(1).to_broadcast([P, 4, KEY]),
                 op=ALU.add,
             )
-            nc.scalar.activation(out=qk_s[:, ms, :], in_=qk_s[:, ms, :], func=ACT.Silu)
+
+        def siluq(h):
+            nc.scalar.activation(
+                out=qk_s[:, 4 * h : 4 * h + 4, :], in_=qk_s[:, 4 * h : 4 * h + 4, :], func=ACT.Silu
+            )
+
+        def rotary(h):
+            ms = slice(4 * h, 4 * h + 4)
             lin = rot.tile([P, 4, 2, KEY], F32, name="lin")
             nc.gpsimd.tensor_tensor(
                 out=lin[:],
@@ -269,9 +444,57 @@ def tile_gau_ae_pa_kernel(
             nc.gpsimd.tensor_tensor(out=hi, in0=ev, in1=sn, op=ALU.mult)
             nc.gpsimd.tensor_tensor(out=t2[:], in0=od, in1=cs, op=ALU.mult)
             nc.gpsimd.tensor_tensor(out=hi, in0=hi, in1=t2[:], op=ALU.add)
-        for s in range(2):
-            nc.gpsimd.dma_start(out=qk_dram[s], in_=ro[:, s].rearrange("p m f -> p (m f)"))
 
-        for sc in range(2):
-            for m in range(MT):
-                step(sc, m, 4 if (sc == 1 and m == MT - 1) else 1)
+        def store_qk():
+            for s in range(2):
+                nc.gpsimd.dma_start(out=qk_dram[s], in_=ro[:, s].rearrange("p m f -> p (m f)"))
+
+        rot_done = []
+        for f in ORDER:
+            op = f[0]
+            if op == "head":
+                head()
+            elif op == "warmSin":
+                warm(ACT.Sin)
+            elif op == "warmSilu":
+                warm(ACT.Silu)
+            elif op == "ldW":
+                load_w(f[1], f[2])
+            elif op == "ldH":
+                load_h(f[1])
+            elif op == "tabV":
+                tab_v()
+            elif op == "tabS":
+                tab_s()
+            elif op == "biasM":
+                bias_m()
+            elif op == "bc":
+                bias_c(f[1])
+            elif op == "trH":
+                tr_h(f[1])
+            elif op == "exH":
+                ex_h(f[1])
+            elif op == "qH":
+                q_h(f[1])
+            elif op == "cp":
+                cp(f[1], f[2], f[3])
+            elif op == "q":
+                quant(f[1], f[2])
+            elif op == "mx":
+                mx(f[1], f[2])
+            elif op == "add":
+                add(f[1], f[2])
+            elif op == "silu":
+                silu(f[1], f[2], f[3])
+            elif op == "mxq":
+                mxq(f[1])
+            elif op == "addq":
+                addq(f[1])
+            elif op == "siluq":
+                siluq(f[1])
+            else:
+                assert op == "rot"
+                rotary(f[1])
+                rot_done.append(f)
+                if len(rot_done) == 2:
+                    store_qk()

@@ -23,148 +23,11 @@ WI = 2 * UV + KEY
 MT = TOK // P
 NG = DIM // 512
 CH = 512
-BLK = 1024
+BLK = 2 * CH
+NBLK = 2 * UV // BLK
 NVEC = WI // P + 4
 
 FLOPS = 2 * TOK * DIM * WI
-
-PINNED = True
-
-ORDER = (
-    ("head",),
-    ("warmSin",),
-    ("ldW", 0, 0),
-    ("ldW", 0, 1),
-    ("ldH", 0),
-    ("ldH", 1),
-    ("ldW", 1, 0),
-    ("ldW", 1, 1),
-    ("ldW", 2, 0),
-    ("ldW", 2, 1),
-    ("ldW", 3, 0),
-    ("ldW", 3, 1),
-    ("tabV",),
-    ("biasM",),
-    ("bc", 0),
-    ("bc", 1),
-    ("bc", 2),
-    ("bc", 3),
-    ("bc", 4),
-    ("tabS",),
-    ("warmSilu",),
-    ("cp", 0, 0, "V"),
-    ("cp", 1, 0, "V"),
-    ("q", 0, 0),
-    ("q", 1, 0),
-    ("cp", 0, 1, "V"),
-    ("cp", 1, 1, "V"),
-    ("q", 0, 1),
-    ("q", 1, 1),
-    ("trH", 0),
-    ("trH", 1),
-    ("trH", 2),
-    ("trH", 3),
-    ("exH", 0),
-    ("exH", 1),
-    ("qH", 0),
-    ("exH", 2),
-    ("exH", 3),
-    ("qH", 1),
-    ("trH", 4),
-    ("trH", 5),
-    ("trH", 6),
-    ("trH", 7),
-    ("exH", 4),
-    ("exH", 5),
-    ("qH", 2),
-    ("exH", 6),
-    ("exH", 7),
-    ("qH", 3),
-    ("mx", 0, 0),
-    ("mx", 0, 1),
-    ("add", 0, 0),
-    ("mx", 0, 2),
-    ("cp", 2, 1, "S"),
-    ("cp", 3, 1, "S"),
-    ("cp", 2, 0, "V"),
-    ("cp", 3, 0, "V"),
-    ("q", 2, 0),
-    ("q", 3, 0),
-    ("silu", 0, 0, 1),
-    ("add", 0, 1),
-    ("mx", 0, 3),
-    ("q", 2, 1),
-    ("q", 3, 1),
-    ("cp", 4, 1, "S"),
-    ("cp", 5, 1, "S"),
-    ("cp", 4, 0, "V"),
-    ("cp", 5, 0, "V"),
-    ("q", 4, 0),
-    ("q", 5, 0),
-    ("silu", 0, 1, 1),
-    ("add", 0, 2),
-    ("mx", 1, 0),
-    ("q", 4, 1),
-    ("q", 5, 1),
-    ("cp", 6, 1, "S"),
-    ("cp", 7, 1, "S"),
-    ("cp", 6, 0, "V"),
-    ("cp", 7, 0, "V"),
-    ("q", 6, 0),
-    ("q", 7, 0),
-    ("silu", 0, 2, 1),
-    ("add", 0, 3),
-    ("cp", 8, 0, "V"),
-    ("cp", 8, 1, "V"),
-    ("q", 6, 1),
-    ("q", 7, 1),
-    ("q", 8, 0),
-    ("q", 8, 1),
-    ("mxq", 0),
-    ("mxq", 1),
-    ("addq", 0),
-    ("addq", 1),
-    ("silu", 0, 3, 1),
-    ("siluq", 0),
-    ("rot", 0),
-    ("siluq", 1),
-    ("rot", 1),
-    ("add", 1, 0),
-    ("mx", 1, 1),
-    ("mx", 1, 2),
-    ("silu", 1, 0, 1),
-    ("add", 1, 1),
-    ("mx", 1, 3),
-    ("silu", 1, 1, 1),
-    ("add", 1, 2),
-    ("mx", 2, 0),
-    ("silu", 1, 2, 1),
-    ("add", 1, 3),
-    ("mx", 2, 1),
-    ("silu", 1, 3, 1),
-    ("add", 2, 0),
-    ("mx", 2, 2),
-    ("silu", 2, 0, 1),
-    ("add", 2, 1),
-    ("mx", 2, 3),
-    ("silu", 2, 1, 1),
-    ("add", 2, 2),
-    ("mx", 3, 0),
-    ("silu", 2, 2, 1),
-    ("add", 2, 3),
-    ("mx", 3, 1),
-    ("silu", 2, 3, 1),
-    ("add", 3, 0),
-    ("mx", 3, 2),
-    ("silu", 3, 0, 1),
-    ("add", 3, 1),
-    ("mx", 3, 3),
-    ("silu", 3, 1, 1),
-    ("add", 3, 2),
-    ("silu", 3, 2, 1),
-    ("add", 3, 3),
-    ("silu", 3, 3, 4),
-)
 
 
 def tile_gau_ae_pa_kernel(
@@ -180,174 +43,136 @@ def tile_gau_ae_pa_kernel(
         out_2.flatten_outer_dims().rearrange("(p m) f -> p (m f)", m=MT),
         out_3.flatten_outer_dims().rearrange("(p m) f -> p (m f)", m=MT),
     ]
-    blocks = [(0, 1024), (1024, 1024), (2048, 1024), (3072, 1152)]
 
     with ExitStack() as ctx:
         const = ctx.enter_context(tc.tile_pool(name="const", bufs=1))
-        rawp = ctx.enter_context(tc.tile_pool(name="rawp", bufs=3))
+        rawp = ctx.enter_context(tc.tile_pool(name="rawp", bufs=1))
         grp = ctx.enter_context(tc.tile_pool(name="grp", bufs=2))
         stage = ctx.enter_context(tc.tile_pool(name="stage", bufs=4))
         rot = ctx.enter_context(tc.tile_pool(name="rot", bufs=2))
         psum = ctx.enter_context(tc.psum_pool(name="psum", bufs=8))
-        if PINNED:
-            ctx.enter_context(tc.manual_schedule())
+        ctx.enter_context(tc.manual_schedule())
 
+        zero1 = const.tile([P, 1], F32, name="zero1")
+        nc.gpsimd.memset(zero1[:], 0.0)
+        scrap = const.tile([P, 1], F32, name="scrap")
+        nc.scalar.activation(out=scrap[:], in_=zero1[:], func=ACT.Sin)
         vecs = const.tile([P, P], BF16, name="vecs")
+        nc.gpsimd.memset(vecs[:], 0.0)
+        nc.sync.dma_start(out=vecs[0 : WI // P, :], in_=bi.rearrange("(r n) -> r n", n=P))
+        for i, v in enumerate((q_gamma, q_beta, k_gamma, k_beta)):
+            r = WI // P + i
+            nc.sync.dma_start(out=vecs[r : r + 1, :], in_=v.rearrange("(o n) -> o n", o=1))
         ident_bf = const.tile([P, P], BF16, name="ident_bf")
-        ident = const.tile([P, P], F32, name="ident")
+        make_identity(nc, ident_bf[:])
         pos = const.tile([P, MT], F32, name="pos")
+        nc.gpsimd.iota(
+            pos[:], pattern=[[1, MT]], base=0, channel_multiplier=MT,
+            allow_small_or_imprecise_dtypes=True,
+        )
+        ident = const.tile([P, P], F32, name="ident")
+        make_identity(nc, ident[:])
+
+        def load_w(c0, width, name):
+            raw = rawp.tile([P, NG, 4, width], BF16, name=name)
+            for g in range(NG):
+                for u in range(2):
+                    r0 = 512 * g + 256 * u
+                    nc.sync.dma_start(
+                        out=raw[:, g, 2 * u : 2 * u + 2, :],
+                        in_=Wi[r0 : r0 + 256, c0 : c0 + width].rearrange("(q e) c -> q e c", e=2),
+                    )
+            return raw
+
+        raws = [load_w(0, BLK, "raw0")]
+        h_half = []
+        for i in range(2):
+            hh = stage.tile([P, MT // 2, DIM], BF16, name="hh%d" % i, tag="st")
+            nc.sync.dma_start(out=hh[:], in_=h_dram[:, 4 * i : 4 * i + 4, :])
+            h_half.append(hh)
+        raw_qk = load_w(2 * UV, KEY, "raw_qk")
+        for b in range(1, NBLK):
+            raws.append(load_w(b * BLK, BLK, "raw%d" % b))
+
         omega = const.tile([P, HALF], F32, name="omega")
+        nc.vector.memset(omega[:, 0:1], 1.0)
+        ratio = 10000.0 ** (-1.0 / HALF)
+        for i in range(6):
+            n = 2 ** i
+            nc.vector.tensor_scalar(
+                out=omega[:, n : 2 * n], in0=omega[:, 0:n], scalar1=ratio ** n, scalar2=None,
+                op0=ALU.mult,
+            )
         turns = const.tile([P, MT, HALF], F32, name="turns")
+        nc.vector.scalar_tensor_tensor(
+            out=turns[:],
+            in0=omega[:].unsqueeze(1).to_broadcast([P, MT, HALF]),
+            scalar=1.0 / (2.0 * math.pi),
+            in1=pos[:].unsqueeze(2).to_broadcast([P, MT, HALF]),
+            op0=ALU.mult, op1=ALU.mult,
+        )
         whole_i = const.tile([P, MT, HALF], I32, name="whole_i")
+        nc.vector.tensor_copy(out=whole_i[:], in_=turns[:])
         whole = const.tile([P, MT, HALF], F32, name="whole")
-        sin_t = const.tile([P, MT, HALF], F32, name="sin_t")
-        cos_t = const.tile([P, MT, HALF], F32, name="cos_t")
+        nc.vector.tensor_copy(out=whole[:], in_=whole_i[:])
+        nc.vector.tensor_tensor(out=turns[:], in0=turns[:], in1=whole[:], op=ALU.subtract)
+        nc.vector.scalar_tensor_tensor(
+            out=whole[:], in0=turns[:], scalar=0.5, in1=turns[:], op0=ALU.is_gt, op1=ALU.subtract,
+        )
+
         spread = const.tile([P, NVEC * P], BF16, name="spread")
+        for b0 in range(0, NVEC, 8):
+            n = min(8, NVEC - b0)
+            bank_bf = psum.tile([P, 8 * P], BF16, name="bank_bf", tag="bank")
+            for r in range(n):
+                nc.tensor.matmul(
+                    out=bank_bf[:, r * P : (r + 1) * P],
+                    lhsT=ident_bf[:, b0 + r : b0 + r + 1].to_broadcast([P, P]),
+                    rhs=vecs[:],
+                    start=True, stop=True,
+                )
+            nc.scalar.copy(out=spread[:, b0 * P : (b0 + n) * P], in_=bank_bf[:, 0 : n * P])
+        gains = spread[:, WI : WI + 4 * P].rearrange("p (s w f) -> p s w f", s=2, w=2)
+
+        sin_t = const.tile([P, MT, HALF], F32, name="sin_t")
+        nc.scalar.activation(out=sin_t[:], in_=whole[:], func=ACT.Sin, scale=-2.0 * math.pi)
+        nc.scalar.activation(out=turns[:], in_=whole[:], func=ACT.Sin, scale=math.pi)
+        nc.scalar.activation(out=turns[:], in_=turns[:], func=ACT.Square)
+        cos_t = const.tile([P, MT, HALF], F32, name="cos_t")
+        nc.gpsimd.tensor_scalar(
+            out=cos_t[:], in0=turns[:], scalar1=-2.0, scalar2=1.0, op0=ALU.mult, op1=ALU.add,
+        )
+        nc.scalar.activation(out=scrap[:], in_=zero1[:], func=ACT.Silu)
+
         wc = const.tile([P, NG, WI], U32, name="wc", align_bytes=64)
         ws = const.tile([P, NG, WI], U8, name="ws", align_bytes=64)
         hc = const.tile([P, MT, NG, P], U32, name="hc", align_bytes=64)
         hs = const.tile([P, MT, NG, P], U8, name="hs", align_bytes=64)
-        qk_s = const.tile([P, MT, KEY], F32, name="qk_s")
-        ro = const.tile([P, 2, MT, KEY], F32, name="ro")
-        gains = spread[:, WI : WI + 4 * P].rearrange("p (s w f) -> p s w f", s=2, w=2)
 
-        scrap_in = const.tile([P, 1], F32, name="scrap_in")
-        scrap_out = const.tile([P, 1], F32, name="scrap_out")
-
-        live = {}
-
-        def head():
-            nc.gpsimd.memset(scrap_in[:], 0.0)
-            nc.gpsimd.memset(vecs[:], 0.0)
-            nc.sync.dma_start(out=vecs[0 : WI // P, :], in_=bi.rearrange("(r n) -> r n", n=P))
-            for i, v in enumerate((q_gamma, q_beta, k_gamma, k_beta)):
-                r = WI // P + i
-                nc.sync.dma_start(out=vecs[r : r + 1, :], in_=v.rearrange("(o n) -> o n", o=1))
-            make_identity(nc, ident_bf[:])
-            nc.gpsimd.iota(
-                pos[:], pattern=[[1, MT]], base=0, channel_multiplier=MT,
-                allow_small_or_imprecise_dtypes=True,
-            )
-            make_identity(nc, ident[:])
-
-        def warm(func):
-            nc.scalar.activation(out=scrap_out[:], in_=scrap_in[:], func=func)
-
-        def load_w(b, g):
-            c0, width = blocks[b]
-            if ("raw", b) not in live:
-                if b < 3:
-                    raw = rawp.tile([P, NG, 4, width], BF16, name="raw%d" % b, tag="rawa")
-                else:
-                    raw = rawp.tile([P, NG, 4, width], BF16, name="raw%d" % b, tag="rawb", bufs=1)
-                live[("raw", b)] = raw
-            raw = live[("raw", b)]
-            for u in range(2):
-                r0 = 512 * g + 256 * u
-                nc.sync.dma_start(
-                    out=raw[:, g, 2 * u : 2 * u + 2, :],
-                    in_=Wi[r0 : r0 + 256, c0 : c0 + width].rearrange("(q e) c -> q e c", e=2),
-                )
-
-        def load_h(i):
-            hh = stage.tile([P, MT // 2, DIM], BF16, name="hh%d" % i, tag="st")
-            nc.sync.dma_start(out=hh[:], in_=h_dram[:, 4 * i : 4 * i + 4, :])
-            live[("hh", i)] = hh
-
-        def tab_v():
-            nc.vector.memset(omega[:, 0:1], 1.0)
-            ratio = 10000.0 ** (-1.0 / HALF)
-            for i in range(6):
-                n = 2 ** i
-                nc.vector.tensor_scalar(
-                    out=omega[:, n : 2 * n], in0=omega[:, 0:n], scalar1=ratio ** n, scalar2=None,
-                    op0=ALU.mult,
-                )
-            nc.vector.scalar_tensor_tensor(
-                out=turns[:],
-                in0=omega[:].unsqueeze(1).to_broadcast([P, MT, HALF]),
-                scalar=1.0 / (2.0 * math.pi),
-                in1=pos[:].unsqueeze(2).to_broadcast([P, MT, HALF]),
-                op0=ALU.mult, op1=ALU.mult,
-            )
-            nc.vector.tensor_copy(out=whole_i[:], in_=turns[:])
-            nc.vector.tensor_copy(out=whole[:], in_=whole_i[:])
-            nc.vector.tensor_tensor(out=turns[:], in0=turns[:], in1=whole[:], op=ALU.subtract)
-            nc.vector.scalar_tensor_tensor(
-                out=whole[:], in0=turns[:], scalar=0.5, in1=turns[:], op0=ALU.is_gt,
-                op1=ALU.subtract,
-            )
-
-        def tab_s():
-            nc.scalar.activation(out=sin_t[:], in_=whole[:], func=ACT.Sin, scale=-2.0 * math.pi)
-            nc.scalar.activation(out=turns[:], in_=whole[:], func=ACT.Sin, scale=math.pi)
-            nc.scalar.activation(out=turns[:], in_=turns[:], func=ACT.Square)
-            nc.gpsimd.tensor_scalar(
-                out=cos_t[:], in0=turns[:], scalar1=-2.0, scalar2=1.0, op0=ALU.mult, op1=ALU.add,
-            )
-
-        def bias_m():
-            for i in range(5):
-                n = min(8, NVEC - 8 * i)
-                bank_bf = psum.tile([P, 8 * P], BF16, name="bank_bf", tag="bank")
-                for r in range(n):
-                    nc.tensor.matmul(
-                        out=bank_bf[:, r * P : (r + 1) * P],
-                        lhsT=ident_bf[:, 8 * i + r : 8 * i + r + 1].to_broadcast([P, P]),
-                        rhs=vecs[:],
-                        start=True, stop=True,
-                    )
-                live[("bb", i)] = bank_bf
-
-        def bias_c(i):
-            n = min(8, NVEC - 8 * i)
-            nc.scalar.copy(
-                out=spread[:, 8 * i * P : (8 * i + n) * P], in_=live[("bb", i)][:, 0 : n * P]
-            )
-
-        def tr_h(m):
-            xt = psum.tile([P, 2 * NG, P], F32, name="xt", tag="bank")
-            words = live[("hh", m // 4)][:, m % 4, :].bitcast(F32)
-            for s in range(2 * NG):
-                nc.tensor.transpose(xt[:, s, :], words[:, s * P : (s + 1) * P], ident[:])
-            live[("xt", m)] = xt
-
-        def ex_h(m):
-            if ("hg", m // 2) not in live:
-                hg = grp.tile([P, 2, NG, P, 4], BF16, name="hg", align_bytes=64)
-                live[("hg", m // 2)] = hg
-            nc.scalar.copy(
-                out=live[("hg", m // 2)][:, m % 2].bitcast(F32),
-                in_=live[("xt", m)][:].rearrange("p (g u) r -> p g r u", u=2),
-            )
-
-        def q_h(pr):
-            nc.vector.quantize_mx(
-                out=hc[:, 2 * pr : 2 * pr + 2].rearrange("p m g r -> p (m g r)").bitcast(FP8X4),
-                scales=hs[:, 2 * pr : 2 * pr + 2].rearrange("p m g r -> p (m g r)"),
-                in_=live[("hg", pr)][:].rearrange("p i g r t -> p (i g r t)"),
-            )
-
-        def cp(c, g, eng):
-            width = KEY if c == 8 else CH
-            b = min(c // 2, 3)
-            off = c * CH - blocks[b][0]
-            gr = grp.tile([P, width, 4], BF16, name="gr", tag="gr" + eng, align_bytes=64)
+        def regroup(raw, off, width, g, on_scalar):
+            tag = "gr_s" if on_scalar else "gr_v"
+            gr = grp.tile([P, width, 4], BF16, name=tag, tag=tag, align_bytes=64)
             dst = gr[:].rearrange("p (c i) t -> p c t i", i=4)
-            src = live[("raw", b)][:, g, :, off : off + width].rearrange("p t (c i) -> p c t i", i=4)
-            if eng == "S":
+            src = raw[:, g, :, off : off + width].rearrange("p t (c i) -> p c t i", i=4)
+            if on_scalar:
                 nc.scalar.copy(out=dst, in_=src)
             else:
                 nc.vector.tensor_copy(out=dst, in_=src)
-            live[("gr", c, g)] = gr
+            return gr
 
-        def quant(c, g):
-            width = KEY if c == 8 else CH
+        def quantise(gr, c0, width, g):
             nc.vector.quantize_mx(
-                out=wc[:, g, c * CH : c * CH + width].bitcast(FP8X4),
-                scales=ws[:, g, c * CH : c * CH + width],
-                in_=live[("gr", c, g)][:].rearrange("p c t -> p (c t)"),
+                out=wc[:, g, c0 : c0 + width].bitcast(FP8X4),
+                scales=ws[:, g, c0 : c0 + width],
+                in_=gr[:].rearrange("p c t -> p (c t)"),
             )
+
+        def regroup_block(b, g, on_scalar):
+            return [regroup(raws[b], j * CH, CH, g, on_scalar) for j in range(2)]
+
+        def quantise_block(grs, b, g):
+            for j in range(2):
+                quantise(grs[j], b * BLK + j * CH, CH, g)
 
         def mx_group(acc, m, c0, width):
             for g in range(NG):
@@ -361,74 +186,86 @@ def tile_gau_ae_pa_kernel(
                     stop=(g == NG - 1),
                 )
 
-        def mx(bl, pr):
+        def multiply(step):
+            b, pr = step // 4, step % 4
+            banks = []
             for k in range(4):
                 acc = psum.tile([P, CH], F32, name="acc", tag="bank")
-                mx_group(acc[:], 2 * pr + k // 2, bl * BLK + (k % 2) * CH, CH)
-                live[("acc", bl, pr, k)] = acc
+                mx_group(acc[:], 2 * pr + k // 2, b * BLK + (k % 2) * CH, CH)
+                banks.append(acc)
+            return banks
 
-        def add(bl, pr):
+        def add_bias(step, banks):
+            b = step // 4
             st = stage.tile([P, 2, BLK], F32, name="st", tag="st")
-            live[("st", bl, pr)] = st
             for k in range(4):
-                c0 = bl * BLK + (k % 2) * CH
+                cols = slice((k % 2) * CH, (k % 2 + 1) * CH)
                 nc.vector.tensor_tensor(
-                    out=st[:, k // 2, (k % 2) * CH : (k % 2 + 1) * CH],
-                    in0=live[("acc", bl, pr, k)][:], in1=spread[:, c0 : c0 + CH], op=ALU.add,
+                    out=st[:, k // 2, cols], in0=banks[k][:],
+                    in1=spread[:, b * BLK + (k % 2) * CH : b * BLK + (k % 2 + 1) * CH], op=ALU.add,
                 )
+            return st
 
-        def silu(bl, pr, pieces):
-            st = live[("st", bl, pr)]
-            dst = uv_dram[bl // 2]
-            off = (bl % 2) * BLK
+        def silu_store(step, st, pieces):
+            b, pr = step // 4, step % 4
+            dst = uv_dram[b // 2]
+            off = (b % 2) * BLK
             if pieces == 1:
                 nc.scalar.activation(out=st[:], in_=st[:], func=ACT.Silu)
                 nc.sync.dma_start(out=dst[:, 2 * pr : 2 * pr + 2, off : off + BLK], in_=st[:])
             else:
-                w = 2 * BLK // pieces
-                for i in range(pieces):
-                    row = (i * w) // BLK
-                    col = (i * w) % BLK
-                    nc.scalar.activation(
-                        out=st[:, row, col : col + w], in_=st[:, row, col : col + w], func=ACT.Silu
-                    )
+                for k in range(4):
+                    cols = slice((k % 2) * CH, (k % 2 + 1) * CH)
+                    nc.scalar.activation(out=st[:, k // 2, cols], in_=st[:, k // 2, cols], func=ACT.Silu)
                     nc.sync.dma_start(
-                        out=dst[:, 2 * pr + row, off + col : off + col + w],
-                        in_=st[:, row, col : col + w],
+                        out=dst[:, 2 * pr + k // 2, off + (k % 2) * CH : off + (k % 2 + 1) * CH],
+                        in_=st[:, k // 2, cols],
                     )
 
-        def mxq(h):
-            qp = psum.tile([P, 4, KEY], F32, name="qp", tag="bank")
-            for i in range(4):
-                mx_group(qp[:, i, :], 4 * h + i, 2 * UV, KEY)
-            live[("qp", h)] = qp
+        for g in range(NG):
+            quantise_block(regroup_block(0, g, False), 0, g)
 
-        def addq(h):
-            nc.vector.tensor_tensor(
-                out=qk_s[:, 4 * h : 4 * h + 4, :], in0=live[("qp", h)][:],
-                in1=spread[:, 2 * UV : WI].unsqueeze(1).to_broadcast([P, 4, KEY]),
-                op=ALU.add,
-            )
+        for h in range(2):
+            xts = []
+            for m in range(4 * h, 4 * h + 4):
+                xt = psum.tile([P, 2 * NG, P], F32, name="xt", tag="bank")
+                words = h_half[h][:, m % 4, :].bitcast(F32)
+                for s in range(2 * NG):
+                    nc.tensor.transpose(xt[:, s, :], words[:, s * P : (s + 1) * P], ident[:])
+                xts.append(xt)
+            for pr in range(2 * h, 2 * h + 2):
+                hg = grp.tile([P, 2, NG, P, 4], BF16, name="hg", align_bytes=64)
+                for i in range(2):
+                    nc.scalar.copy(
+                        out=hg[:, i].bitcast(F32),
+                        in_=xts[2 * (pr % 2) + i][:].rearrange("p (g u) r -> p g r u", u=2),
+                    )
+                nc.vector.quantize_mx(
+                    out=hc[:, 2 * pr : 2 * pr + 2].rearrange("p m g r -> p (m g r)").bitcast(FP8X4),
+                    scales=hs[:, 2 * pr : 2 * pr + 2].rearrange("p m g r -> p (m g r)"),
+                    in_=hg[:].rearrange("p i g r t -> p (i g r t)"),
+                )
 
-        def siluq(h):
-            nc.scalar.activation(
-                out=qk_s[:, 4 * h : 4 * h + 4, :], in_=qk_s[:, 4 * h : 4 * h + 4, :], func=ACT.Silu
-            )
+        gr_qk = [regroup(raw_qk, 0, KEY, g, False) for g in range(NG)]
+        for g in range(NG):
+            quantise(gr_qk[g], 2 * UV, KEY, g)
+
+        qk_s = const.tile([P, MT, KEY], F32, name="qk_s")
+        ro = const.tile([P, 2, MT, KEY], F32, name="ro")
 
         def rotary(h):
             ms = slice(4 * h, 4 * h + 4)
             lin = rot.tile([P, 4, 2, KEY], F32, name="lin")
-            nc.gpsimd.tensor_tensor(
-                out=lin[:],
-                in0=qk_s[:, ms, :].unsqueeze(2).to_broadcast([P, 4, 2, KEY]),
-                in1=gains[:, :, 0, :].unsqueeze(1).to_broadcast([P, 4, 2, KEY]),
-                op=ALU.mult,
-            )
-            nc.gpsimd.tensor_tensor(
-                out=lin[:], in0=lin[:],
-                in1=gains[:, :, 1, :].unsqueeze(1).to_broadcast([P, 4, 2, KEY]),
-                op=ALU.add,
-            )
+            for s in range(2):
+                nc.gpsimd.tensor_tensor(
+                    out=lin[:, :, s, :], in0=qk_s[:, ms, :],
+                    in1=gains[:, s, 0, :].unsqueeze(1).to_broadcast([P, 4, KEY]), op=ALU.mult,
+                )
+            for s in range(2):
+                nc.gpsimd.tensor_tensor(
+                    out=lin[:, :, s, :], in0=lin[:, :, s, :],
+                    in1=gains[:, s, 1, :].unsqueeze(1).to_broadcast([P, 4, KEY]), op=ALU.add,
+                )
             pairs = lin[:].rearrange("p m s (j e) -> p m s j e", e=2)
             ev = pairs[:, :, :, :, 0]
             od = pairs[:, :, :, :, 1]
@@ -445,56 +282,38 @@ def tile_gau_ae_pa_kernel(
             nc.gpsimd.tensor_tensor(out=t2[:], in0=od, in1=cs, op=ALU.mult)
             nc.gpsimd.tensor_tensor(out=hi, in0=hi, in1=t2[:], op=ALU.add)
 
-        def store_qk():
-            for s in range(2):
-                nc.gpsimd.dma_start(out=qk_dram[s], in_=ro[:, s].rearrange("p m f -> p (m f)"))
-
-        rot_done = []
-        for f in ORDER:
-            op = f[0]
-            if op == "head":
-                head()
-            elif op == "warmSin":
-                warm(ACT.Sin)
-            elif op == "warmSilu":
-                warm(ACT.Silu)
-            elif op == "ldW":
-                load_w(f[1], f[2])
-            elif op == "ldH":
-                load_h(f[1])
-            elif op == "tabV":
-                tab_v()
-            elif op == "tabS":
-                tab_s()
-            elif op == "biasM":
-                bias_m()
-            elif op == "bc":
-                bias_c(f[1])
-            elif op == "trH":
-                tr_h(f[1])
-            elif op == "exH":
-                ex_h(f[1])
-            elif op == "qH":
-                q_h(f[1])
-            elif op == "cp":
-                cp(f[1], f[2], f[3])
-            elif op == "q":
-                quant(f[1], f[2])
-            elif op == "mx":
-                mx(f[1], f[2])
-            elif op == "add":
-                add(f[1], f[2])
-            elif op == "silu":
-                silu(f[1], f[2], f[3])
-            elif op == "mxq":
-                mxq(f[1])
-            elif op == "addq":
-                addq(f[1])
-            elif op == "siluq":
-                siluq(f[1])
-            else:
-                assert op == "rot"
-                rotary(f[1])
-                rot_done.append(f)
-                if len(rot_done) == 2:
-                    store_qk()
+        NSTEP = 4 * NBLK
+        banks = {0: multiply(0)}
+        qps = []
+        for h in range(2):
+            qp = psum.tile([P, 4, KEY], F32, name="qp", tag="bank")
+            for i in range(4):
+                mx_group(qp[:, i, :], 4 * h + i, 2 * UV, KEY)
+            qps.append(qp)
+        late = None
+        for step in range(NSTEP):
+            st = add_bias(step, banks[step])
+            if step == 0:
+                for h in range(2):
+                    nc.vector.tensor_tensor(
+                        out=qk_s[:, 4 * h : 4 * h + 4, :], in0=qps[h][:],
+                        in1=spread[:, 2 * UV : WI].unsqueeze(1).to_broadcast([P, 4, KEY]),
+                        op=ALU.add,
+                    )
+                banks[1] = multiply(1)
+            if step + 2 < NSTEP:
+                banks[step + 2] = multiply(step + 2)
+            if step == 0:
+                for h in range(2):
+                    ms = slice(4 * h, 4 * h + 4)
+                    nc.scalar.activation(out=qk_s[:, ms, :], in_=qk_s[:, ms, :], func=ACT.Silu)
+                    rotary(h)
+                for s in range(2):
+                    nc.gpsimd.dma_start(out=qk_dram[s], in_=ro[:, s].rearrange("p m f -> p (m f)"))
+            if late is not None:
+                quantise_block(late, step, 1)
+                late = None
+            if step + 1 < NBLK:
+                late = regroup_block(step + 1, 1, True)
+                quantise_block(regroup_block(step + 1, 0, False), step + 1, 0)
+            silu_store(step, st, 4 if step == NSTEP - 1 else 1)

@@ -46,10 +46,10 @@ def tile_gau_ae_pa_kernel(
 
     with ExitStack() as ctx:
         const = ctx.enter_context(tc.tile_pool(name="const", bufs=1))
-        rawp = ctx.enter_context(tc.tile_pool(name="rawp", bufs=1))
+        rawp = ctx.enter_context(tc.tile_pool(name="rawp", bufs=3))
         grp = ctx.enter_context(tc.tile_pool(name="grp", bufs=2))
-        stage = ctx.enter_context(tc.tile_pool(name="stage", bufs=4))
-        rot = ctx.enter_context(tc.tile_pool(name="rot", bufs=2))
+        stage = ctx.enter_context(tc.tile_pool(name="stage", bufs=7))
+        rot = ctx.enter_context(tc.tile_pool(name="rot", bufs=1))
         psum = ctx.enter_context(tc.psum_pool(name="psum", bufs=8))
         ctx.enter_context(tc.manual_schedule())
 
@@ -73,8 +73,8 @@ def tile_gau_ae_pa_kernel(
         ident = const.tile([P, P], F32, name="ident")
         make_identity(nc, ident[:])
 
-        def load_w(c0, width, name):
-            raw = rawp.tile([P, NG, 4, width], BF16, name=name)
+        def load_w(c0, width, name, tag, bufs):
+            raw = rawp.tile([P, NG, 4, width], BF16, name=name, tag=tag, bufs=bufs)
             for g in range(NG):
                 for u in range(2):
                     r0 = 512 * g + 256 * u
@@ -84,15 +84,15 @@ def tile_gau_ae_pa_kernel(
                     )
             return raw
 
-        raws = [load_w(0, BLK, "raw0")]
+        raws = [load_w(0, BLK, "raw0", "raw", 3)]
         h_half = []
         for i in range(2):
             hh = stage.tile([P, MT // 2, DIM], BF16, name="hh%d" % i, tag="st")
             nc.sync.dma_start(out=hh[:], in_=h_dram[:, 4 * i : 4 * i + 4, :])
             h_half.append(hh)
-        raw_qk = load_w(2 * UV, KEY, "raw_qk")
-        for b in range(1, NBLK):
-            raws.append(load_w(b * BLK, BLK, "raw%d" % b))
+        raw_qk = load_w(2 * UV, KEY, "raw_qk", "raw_qk", 1)
+        for b in range(1, NBLK - 1):
+            raws.append(load_w(b * BLK, BLK, "raw%d" % b, "raw", 3))
 
         omega = const.tile([P, HALF], F32, name="omega")
         nc.vector.memset(omega[:, 0:1], 1.0)
@@ -224,6 +224,7 @@ def tile_gau_ae_pa_kernel(
 
         for g in range(NG):
             quantise_block(regroup_block(0, g, False), 0, g)
+        raws.append(load_w((NBLK - 1) * BLK, BLK, "raw%d" % (NBLK - 1), "raw", 3))
 
         for h in range(2):
             xts = []

@@ -26,6 +26,8 @@ CH = 512
 BLK = 2 * CH
 NBLK = 2 * UV // BLK
 NVEC = WI // P + 4
+EARLY = BLK // P
+LATE = 2 * UV // P
 
 FLOPS = 2 * TOK * DIM * WI
 
@@ -72,6 +74,8 @@ def tile_gau_ae_pa_kernel(
         )
         ident = const.tile([P, P], F32, name="ident")
         make_identity(nc, ident[:])
+
+        spread = const.tile([P, NVEC * P], BF16, name="spread")
 
         def load_w(c0, width, name, tag, bufs):
             raw = rawp.tile([P, NG, 4, width], BF16, name=name, tag=tag, bufs=bufs)
@@ -120,9 +124,7 @@ def tile_gau_ae_pa_kernel(
             out=whole[:], in0=turns[:], scalar=0.5, in1=turns[:], op0=ALU.is_gt, op1=ALU.subtract,
         )
 
-        spread = const.tile([P, NVEC * P], BF16, name="spread")
-        for b0 in range(0, NVEC, 8):
-            n = min(8, NVEC - b0)
+        def spread_rows(b0, n):
             bank_bf = psum.tile([P, 8 * P], BF16, name="bank_bf", tag="bank")
             for r in range(n):
                 nc.tensor.matmul(
@@ -132,6 +134,9 @@ def tile_gau_ae_pa_kernel(
                     start=True, stop=True,
                 )
             nc.scalar.copy(out=spread[:, b0 * P : (b0 + n) * P], in_=bank_bf[:, 0 : n * P])
+
+        spread_rows(0, EARLY)
+        spread_rows(LATE, NVEC - LATE)
         gains = spread[:, WI : WI + 4 * P].rearrange("p (s w f) -> p s w f", s=2, w=2)
 
         sin_t = const.tile([P, MT, HALF], F32, name="sin_t")
@@ -142,7 +147,6 @@ def tile_gau_ae_pa_kernel(
         nc.gpsimd.tensor_scalar(
             out=cos_t[:], in0=turns[:], scalar1=-2.0, scalar2=1.0, op0=ALU.mult, op1=ALU.add,
         )
-        nc.scalar.activation(out=scrap[:], in_=zero1[:], func=ACT.Silu)
 
         wc = const.tile([P, NG, WI], U32, name="wc", align_bytes=64)
         ws = const.tile([P, NG, WI], U8, name="ws", align_bytes=64)
@@ -206,24 +210,26 @@ def tile_gau_ae_pa_kernel(
                 )
             return st
 
-        def silu_store(step, st, pieces):
+        def silu_store(step, st):
             b, pr = step // 4, step % 4
             dst = uv_dram[b // 2]
             off = (b % 2) * BLK
-            if pieces == 1:
+            if step < NSTEP - 2:
                 nc.scalar.activation(out=st[:], in_=st[:], func=ACT.Silu)
                 nc.sync.dma_start(out=dst[:, 2 * pr : 2 * pr + 2, off : off + BLK], in_=st[:])
-            else:
-                for k in range(4):
-                    cols = slice((k % 2) * CH, (k % 2 + 1) * CH)
-                    nc.scalar.activation(out=st[:, k // 2, cols], in_=st[:, k // 2, cols], func=ACT.Silu)
-                    nc.sync.dma_start(
-                        out=dst[:, 2 * pr + k // 2, off + (k % 2) * CH : off + (k % 2 + 1) * CH],
-                        in_=st[:, k // 2, cols],
-                    )
+                return
+            wide = BLK if step == NSTEP - 2 else CH
+            for i in range(2):
+                for c0 in range(0, BLK, wide):
+                    piece = st[:, i, c0 : c0 + wide]
+                    nc.scalar.activation(out=piece, in_=piece, func=ACT.Silu)
+                    nc.sync.dma_start(out=dst[:, 2 * pr + i, off + c0 : off + c0 + wide], in_=piece)
 
-        for g in range(NG):
-            quantise_block(regroup_block(0, g, False), 0, g)
+        on_scalar = regroup(raws[0], CH, CH, 1, True)
+        quantise_block(regroup_block(0, 0, False), 0, 0)
+        on_vector = regroup(raws[0], 0, CH, 1, False)
+        quantise(on_scalar, CH, CH, 1)
+        quantise(on_vector, 0, CH, 1)
         raws.append(load_w((NBLK - 1) * BLK, BLK, "raw%d" % (NBLK - 1), "raw", 3))
 
         for h in range(2):
@@ -246,6 +252,10 @@ def tile_gau_ae_pa_kernel(
                     scales=hs[:, 2 * pr : 2 * pr + 2].rearrange("p m g r -> p (m g r)"),
                     in_=hg[:].rearrange("p i g r t -> p (i g r t)"),
                 )
+
+        for b in range(1, NBLK):
+            spread_rows(b * EARLY, EARLY)
+        nc.scalar.activation(out=scrap[:], in_=zero1[:], func=ACT.Silu)
 
         gr_qk = [regroup(raw_qk, 0, KEY, g, False) for g in range(NG)]
         for g in range(NG):
@@ -317,4 +327,4 @@ def tile_gau_ae_pa_kernel(
             if step + 1 < NBLK:
                 late = regroup_block(step + 1, 1, True)
                 quantise_block(regroup_block(step + 1, 0, False), step + 1, 0)
-            silu_store(step, st, 4 if step == NSTEP - 1 else 1)
+            silu_store(step, st)

import math
from contextlib import ExitStack

import concourse.mybir as mybir
from concourse.masks import make_identity

F32 = mybir.dt.float32
BF16 = mybir.dt.bfloat16
I32 = mybir.dt.int32
U32 = mybir.dt.uint32
U8 = mybir.dt.uint8
FP8X4 = mybir.dt.float8_e4m3fn_x4
ALU = mybir.AluOpType
ACT = mybir.ActivationFunctionType

P = 128
TOK = 1024
DIM = 1024
UV = 2048
KEY = 128
HALF = KEY // 2
WI = 2 * UV + KEY
MT = TOK // P
NG = DIM // 512
CH = 512
BLK = 2 * CH
NBLK = 2 * UV // BLK
NVEC = WI // P + 4
EARLY = BLK // P
LATE = 2 * UV // P

FLOPS = 2 * TOK * DIM * WI


def tile_gau_ae_pa_kernel(
    tc, hidden_states, Wi, bi, q_gamma, q_beta, k_gamma, k_beta, out_0, out_1, out_2, out_3
):
    nc = tc.nc
    h_dram = hidden_states.flatten_outer_dims().rearrange("(p m) k -> p m k", m=MT)
    uv_dram = [
        out_0.flatten_outer_dims().rearrange("(p m) c -> p m c", m=MT),
        out_1.flatten_outer_dims().rearrange("(p m) c -> p m c", m=MT),
    ]
    qk_dram = [
        out_2.flatten_outer_dims().rearrange("(p m) f -> p (m f)", m=MT),
        out_3.flatten_outer_dims().rearrange("(p m) f -> p (m f)", m=MT),
    ]

    with ExitStack() as ctx:
        const = ctx.enter_context(tc.tile_pool(name="const", bufs=1))
        rawp = ctx.enter_context(tc.tile_pool(name="rawp", bufs=3))
        grp = ctx.enter_context(tc.tile_pool(name="grp", bufs=2))
        stage = ctx.enter_context(tc.tile_pool(name="stage", bufs=7))
        rot = ctx.enter_context(tc.tile_pool(name="rot", bufs=1))
        psum = ctx.enter_context(tc.psum_pool(name="psum", bufs=8))
        ctx.enter_context(tc.manual_schedule())

        zero1 = const.tile([P, 1], F32, name="zero1")
        nc.gpsimd.memset(zero1[:], 0.0)
        scrap = const.tile([P, 1], F32, name="scrap")
        nc.scalar.activation(out=scrap[:], in_=zero1[:], func=ACT.Sin)
        vecs = const.tile([P, P], BF16, name="vecs")
        nc.gpsimd.memset(vecs[:], 0.0)
        nc.sync.dma_start(out=vecs[0 : WI // P, :], in_=bi.rearrange("(r n) -> r n", n=P))
        for i, v in enumerate((q_gamma, q_beta, k_gamma, k_beta)):
            r = WI // P + i
            nc.sync.dma_start(out=vecs[r : r + 1, :], in_=v.rearrange("(o n) -> o n", o=1))
        ident_bf = const.tile([P, P], BF16, name="ident_bf")
        make_identity(nc, ident_bf[:])
        pos = const.tile([P, MT], F32, name="pos")
        nc.gpsimd.iota(
            pos[:], pattern=[[1, MT]], base=0, channel_multiplier=MT,
            allow_small_or_imprecise_dtypes=True,
        )
        ident = const.tile([P, P], F32, name="ident")
        make_identity(nc, ident[:])

        spread = const.tile([P, NVEC * P], BF16, name="spread")

        def load_w(c0, width, name, tag, bufs):
            raw = rawp.tile([P, NG, 4, width], BF16, name=name, tag=tag, bufs=bufs)
            for g in range(NG):
                for u in range(2):
                    r0 = 512 * g + 256 * u
                    nc.sync.dma_start(
                        out=raw[:, g, 2 * u : 2 * u + 2, :],
                        in_=Wi[r0 : r0 + 256, c0 : c0 + width].rearrange("(q e) c -> q e c", e=2),
                    )
            return raw

        raws = [load_w(0, BLK, "raw0", "raw", 3)]
        h_half = []
        for i in range(2):
            hh = stage.tile([P, MT // 2, DIM], BF16, name="hh%d" % i, tag="st")
            nc.sync.dma_start(out=hh[:], in_=h_dram[:, 4 * i : 4 * i + 4, :])
            h_half.append(hh)
        raw_qk = load_w(2 * UV, KEY, "raw_qk", "raw_qk", 1)
        for b in range(1, NBLK - 1):
            raws.append(load_w(b * BLK, BLK, "raw%d" % b, "raw", 3))

        omega = const.tile([P, HALF], F32, name="omega")
        nc.vector.memset(omega[:, 0:1], 1.0)
        ratio = 10000.0 ** (-1.0 / HALF)
        for i in range(6):
            n = 2 ** i
            nc.vector.tensor_scalar(
                out=omega[:, n : 2 * n], in0=omega[:, 0:n], scalar1=ratio ** n, scalar2=None,
                op0=ALU.mult,
            )
        turns = const.tile([P, MT, HALF], F32, name="turns")
        nc.vector.scalar_tensor_tensor(
            out=turns[:],
            in0=omega[:].unsqueeze(1).to_broadcast([P, MT, HALF]),
            scalar=1.0 / (2.0 * math.pi),
            in1=pos[:].unsqueeze(2).to_broadcast([P, MT, HALF]),
            op0=ALU.mult, op1=ALU.mult,
        )
        whole_i = const.tile([P, MT, HALF], I32, name="whole_i")
        nc.vector.tensor_copy(out=whole_i[:], in_=turns[:])
        whole = const.tile([P, MT, HALF], F32, name="whole")
        nc.vector.tensor_copy(out=whole[:], in_=whole_i[:])
        nc.vector.tensor_tensor(out=turns[:], in0=turns[:], in1=whole[:], op=ALU.subtract)
        nc.vector.scalar_tensor_tensor(
            out=whole[:], in0=turns[:], scalar=0.5, in1=turns[:], op0=ALU.is_gt, op1=ALU.subtract,
        )

        def spread_rows(b0, n):
            bank_bf = psum.tile([P, 8 * P], BF16, name="bank_bf", tag="bank")
            for r in range(n):
                nc.tensor.matmul(
                    out=bank_bf[:, r * P : (r + 1) * P],
                    lhsT=ident_bf[:, b0 + r : b0 + r + 1].to_broadcast([P, P]),
                    rhs=vecs[:],
                    start=True, stop=True,
                )
            nc.scalar.copy(out=spread[:, b0 * P : (b0 + n) * P], in_=bank_bf[:, 0 : n * P])

        spread_rows(0, EARLY)
        spread_rows(LATE, NVEC - LATE)
        gains = spread[:, WI : WI + 4 * P].rearrange("p (s w f) -> p s w f", s=2, w=2)

        sin_t = const.tile([P, MT, HALF], F32, name="sin_t")
        nc.scalar.activation(out=sin_t[:], in_=whole[:], func=ACT.Sin, scale=-2.0 * math.pi)
        nc.scalar.activation(out=turns[:], in_=whole[:], func=ACT.Sin, scale=math.pi)
        nc.scalar.activation(out=turns[:], in_=turns[:], func=ACT.Square)
        cos_t = const.tile([P, MT, HALF], F32, name="cos_t")
        nc.gpsimd.tensor_scalar(
            out=cos_t[:], in0=turns[:], scalar1=-2.0, scalar2=1.0, op0=ALU.mult, op1=ALU.add,
        )

        wc = const.tile([P, NG, WI], U32, name="wc", align_bytes=64)
        ws = const.tile([P, NG, WI], U8, name="ws", align_bytes=64)
        hc = const.tile([P, MT, NG, P], U32, name="hc", align_bytes=64)
        hs = const.tile([P, MT, NG, P], U8, name="hs", align_bytes=64)

        def regroup(raw, off, width, g, on_scalar):
            tag = "gr_s" if on_scalar else "gr_v"
            gr = grp.tile([P, width, 4], BF16, name=tag, tag=tag, align_bytes=64)
            dst = gr[:].rearrange("p (c i) t -> p c t i", i=4)
            src = raw[:, g, :, off : off + width].rearrange("p t (c i) -> p c t i", i=4)
            if on_scalar:
                nc.scalar.copy(out=dst, in_=src)
            else:
                nc.vector.tensor_copy(out=dst, in_=src)
            return gr

        def quantise(gr, c0, width, g):
            nc.vector.quantize_mx(
                out=wc[:, g, c0 : c0 + width].bitcast(FP8X4),
                scales=ws[:, g, c0 : c0 + width],
                in_=gr[:].rearrange("p c t -> p (c t)"),
            )

        def regroup_block(b, g, on_scalar):
            return [regroup(raws[b], j * CH, CH, g, on_scalar) for j in range(2)]

        def quantise_block(grs, b, g):
            for j in range(2):
                quantise(grs[j], b * BLK + j * CH, CH, g)

        def mx_group(acc, m, c0, width):
            for g in range(NG):
                nc.tensor.matmul_mx(
                    out=acc,
                    lhsT=hc[:, m, g, :].bitcast(FP8X4),
                    lhsT_scale=hs[:, m, g, :],
                    rhs=wc[:, g, c0 : c0 + width].bitcast(FP8X4),
                    rhs_scale=ws[:, g, c0 : c0 + width],
                    start=(g == 0),
                    stop=(g == NG - 1),
                )

        def multiply(step):
            b, pr = step // 4, step % 4
            banks = []
            for k in range(4):
                acc = psum.tile([P, CH], F32, name="acc", tag="bank")
                mx_group(acc[:], 2 * pr + k // 2, b * BLK + (k % 2) * CH, CH)
                banks.append(acc)
            return banks

        def add_bias(step, banks):
            b = step // 4
            st = stage.tile([P, 2, BLK], F32, name="st", tag="st")
            for k in range(4):
                cols = slice((k % 2) * CH, (k % 2 + 1) * CH)
                nc.vector.tensor_tensor(
                    out=st[:, k // 2, cols], in0=banks[k][:],
                    in1=spread[:, b * BLK + (k % 2) * CH : b * BLK + (k % 2 + 1) * CH], op=ALU.add,
                )
            return st

        def silu_store(step, st):
            b, pr = step // 4, step % 4
            dst = uv_dram[b // 2]
            off = (b % 2) * BLK
            if step < NSTEP - 2:
                nc.scalar.activation(out=st[:], in_=st[:], func=ACT.Silu)
                nc.sync.dma_start(out=dst[:, 2 * pr : 2 * pr + 2, off : off + BLK], in_=st[:])
                return
            wide = BLK if step == NSTEP - 2 else CH
            for i in range(2):
                for c0 in range(0, BLK, wide):
                    piece = st[:, i, c0 : c0 + wide]
                    nc.scalar.activation(out=piece, in_=piece, func=ACT.Silu)
                    nc.sync.dma_start(out=dst[:, 2 * pr + i, off + c0 : off + c0 + wide], in_=piece)

        on_scalar = regroup(raws[0], CH, CH, 1, True)
        quantise_block(regroup_block(0, 0, False), 0, 0)
        on_vector = regroup(raws[0], 0, CH, 1, False)
        quantise(on_scalar, CH, CH, 1)
        quantise(on_vector, 0, CH, 1)
        raws.append(load_w((NBLK - 1) * BLK, BLK, "raw%d" % (NBLK - 1), "raw", 3))

        for h in range(2):
            xts = []
            for m in range(4 * h, 4 * h + 4):
                xt = psum.tile([P, 2 * NG, P], F32, name="xt", tag="bank")
                words = h_half[h][:, m % 4, :].bitcast(F32)
                for s in range(2 * NG):
                    nc.tensor.transpose(xt[:, s, :], words[:, s * P : (s + 1) * P], ident[:])
                xts.append(xt)
            for pr in range(2 * h, 2 * h + 2):
                hg = grp.tile([P, 2, NG, P, 4], BF16, name="hg", align_bytes=64)
                for i in range(2):
                    nc.scalar.copy(
                        out=hg[:, i].bitcast(F32),
                        in_=xts[2 * (pr % 2) + i][:].rearrange("p (g u) r -> p g r u", u=2),
                    )
                nc.vector.quantize_mx(
                    out=hc[:, 2 * pr : 2 * pr + 2].rearrange("p m g r -> p (m g r)").bitcast(FP8X4),
                    scales=hs[:, 2 * pr : 2 * pr + 2].rearrange("p m g r -> p (m g r)"),
                    in_=hg[:].rearrange("p i g r t -> p (i g r t)"),
                )

        for b in range(1, NBLK):
            spread_rows(b * EARLY, EARLY)
        nc.scalar.activation(out=scrap[:], in_=zero1[:], func=ACT.Silu)

        gr_qk = [regroup(raw_qk, 0, KEY, g, False) for g in range(NG)]
        for g in range(NG):
            quantise(gr_qk[g], 2 * UV, KEY, g)

        qk_s = const.tile([P, MT, KEY], F32, name="qk_s")
        ro = const.tile([P, 2, MT, KEY], F32, name="ro")

        def rotary(h):
            ms = slice(4 * h, 4 * h + 4)
            lin = rot.tile([P, 4, 2, KEY], F32, name="lin")
            for s in range(2):
                nc.gpsimd.tensor_tensor(
                    out=lin[:, :, s, :], in0=qk_s[:, ms, :],
                    in1=gains[:, s, 0, :].unsqueeze(1).to_broadcast([P, 4, KEY]), op=ALU.mult,
                )
            for s in range(2):
                nc.gpsimd.tensor_tensor(
                    out=lin[:, :, s, :], in0=lin[:, :, s, :],
                    in1=gains[:, s, 1, :].unsqueeze(1).to_broadcast([P, 4, KEY]), op=ALU.add,
                )
            pairs = lin[:].rearrange("p m s (j e) -> p m s j e", e=2)
            ev = pairs[:, :, :, :, 0]
            od = pairs[:, :, :, :, 1]
            cs = cos_t[:, ms, :].unsqueeze(2).to_broadcast([P, 4, 2, HALF])
            sn = sin_t[:, ms, :].unsqueeze(2).to_broadcast([P, 4, 2, HALF])
            lo = ro[:, :, ms, 0:HALF].rearrange("p s m j -> p m s j")
            hi = ro[:, :, ms, HALF:KEY].rearrange("p s m j -> p m s j")
            t1 = rot.tile([P, 4, 2, HALF], F32, name="t1")
            t2 = rot.tile([P, 4, 2, HALF], F32, name="t2")
            nc.gpsimd.tensor_tensor(out=lo, in0=ev, in1=cs, op=ALU.mult)
            nc.gpsimd.tensor_tensor(out=t1[:], in0=od, in1=sn, op=ALU.mult)
            nc.gpsimd.tensor_tensor(out=lo, in0=lo, in1=t1[:], op=ALU.subtract)
            nc.gpsimd.tensor_tensor(out=hi, in0=ev, in1=sn, op=ALU.mult)
            nc.gpsimd.tensor_tensor(out=t2[:], in0=od, in1=cs, op=ALU.mult)
            nc.gpsimd.tensor_tensor(out=hi, in0=hi, in1=t2[:], op=ALU.add)

        NSTEP = 4 * NBLK
        banks = {0: multiply(0)}
        qps = []
        for h in range(2):
            qp = psum.tile([P, 4, KEY], F32, name="qp", tag="bank")
            for i in range(4):
                mx_group(qp[:, i, :], 4 * h + i, 2 * UV, KEY)
            qps.append(qp)
        late = None
        for step in range(NSTEP):
            st = add_bias(step, banks[step])
            if step == 0:
                for h in range(2):
                    nc.vector.tensor_tensor(
                        out=qk_s[:, 4 * h : 4 * h + 4, :], in0=qps[h][:],
                        in1=spread[:, 2 * UV : WI].unsqueeze(1).to_broadcast([P, 4, KEY]),
                        op=ALU.add,
                    )
                banks[1] = multiply(1)
            if step + 2 < NSTEP:
                banks[step + 2] = multiply(step + 2)
            if step == 0:
                for h in range(2):
                    ms = slice(4 * h, 4 * h + 4)
                    nc.scalar.activation(out=qk_s[:, ms, :], in_=qk_s[:, ms, :], func=ACT.Silu)
                    rotary(h)
                for s in range(2):
                    nc.gpsimd.dma_start(out=qk_dram[s], in_=ro[:, s].rearrange("p m f -> p (m f)"))
            if late is not None:
                quantise_block(late, step, 1)
                late = None
            if step + 1 < NBLK:
                late = regroup_block(step + 1, 1, True)
                quantise_block(regroup_block(step + 1, 0, False), step + 1, 0)
            silu_store(step, st)
